import numpy as np
import ml_dtypes

BF16 = ml_dtypes.bfloat16


def bf(x):
    return np.asarray(x, np.float32).astype(BF16)


def f32(x):
    return np.asarray(x, np.float32)


def f64(x):
    return np.asarray(x).astype(np.float64)


def striped(idx):
    return np.tile(idx.reshape(-1, 16).T, (8, 1))


D, S, N, P, T = 128, 1024, 2048, 1024, 2
BC2 = 0.25


def setup_inputs():
    return {
        "table": bf(np.random.standard_normal((D, S))),
        "w": bf(np.random.standard_normal((D, D)) / np.sqrt(D)),
        "b1": f32(0.1 * np.random.standard_normal((D, 1))),
        "bd": bf(np.random.standard_normal((D, D)) * np.sqrt(2.0 / D)),
        "boff": f32(0.1 * np.random.standard_normal((D, 1))),
        "wc1": bf(np.random.standard_normal((D, D)) * np.sqrt(2.0 / D)),
        "bc1": f32(0.1 * np.random.standard_normal((D, 1))),
        "wc2": bf(np.random.standard_normal((D, 1)) * np.sqrt(2.0 / D)),
        "phenos": f32(np.random.standard_normal((T, P))),
        "offs": striped(np.random.permutation(np.tile(np.arange(S), 2))[:N]),
    }


def reference(table, w, b1, bd, boff, wc1, bc1, wc2, phenos, offs):
    idx = offs[:16].T.reshape(-1)
    h = np.maximum(f64(w).T @ f64(table)[:, idx] + f64(b1), 0.0)
    e0, e1 = h[:, :P], h[:, P:]
    z = e1 * (f64(bd).T @ e0) + f64(boff)
    y = np.maximum(f64(wc1).T @ z + f64(bc1), 0.0)
    return (f64(wc2) * y).sum(axis=0, keepdims=True) + f64(phenos).sum(axis=0, keepdims=True) + BC2

@@ -1,0 +1,80 @@
+import concourse.mybir as mybir
+
+BF16, F32, U16 = mybir.dt.bfloat16, mybir.dt.float32, mybir.dt.uint16
+RELU = mybir.ActivationFunctionType.Relu
+ADD, MULT, MAX = mybir.AluOpType.add, mybir.AluOpType.mult, mybir.AluOpType.max
+
+D = 128
+GENES = 1024
+PAIRS = 1024
+PIECE = 512
+HALVES = PAIRS // PIECE
+BC2 = 0.25
+
+FLOPS = 2 * D * D * (2 * PAIRS) + 2 * (2 * D * D * PAIRS) + 2 * D * PAIRS
+
+
+def tile_recovermodel_kernel(tc, table, w, b1, bd, boff, wc1, bc1, wc2, phenos, offs, out):
+    nc = tc.nc
+    with (
+        tc.tile_pool(name="held", bufs=1) as held,
+        tc.tile_pool(name="work", bufs=2) as work,
+        tc.psum_pool(name="psum", bufs=8) as psum,
+    ):
+        offsets = held.tile([D, 2 * PAIRS // 16], U16, name="offsets")
+        nc.sync.dma_start(offsets[:], offs)
+        table_sb = held.tile([D, GENES], BF16, name="table_sb")
+        nc.sync.dma_start(table_sb[:], table)
+        w_sb = held.tile([D, D], BF16, name="w_sb")
+        nc.scalar.dma_start(w_sb[:], w)
+        bd_sb = held.tile([D, D], BF16, name="bd_sb")
+        nc.scalar.dma_start(bd_sb[:], bd)
+        wc1_sb = held.tile([D, D], BF16, name="wc1_sb")
+        nc.scalar.dma_start(wc1_sb[:], wc1)
+        b1_sb = held.tile([D, 1], F32, name="b1_sb")
+        nc.gpsimd.dma_start(b1_sb[:], b1)
+        boff_sb = held.tile([D, 1], F32, name="boff_sb")
+        nc.gpsimd.dma_start(boff_sb[:], boff)
+        bc1_sb = held.tile([D, 1], F32, name="bc1_sb")
+        nc.gpsimd.dma_start(bc1_sb[:], bc1)
+        wc2_sb = held.tile([D, 1], BF16, name="wc2_sb")
+        nc.gpsimd.dma_start(wc2_sb[:], wc2)
+        phenos_sb = held.tile([1, 2 * PAIRS], F32, name="phenos_sb")
+        nc.gpsimd.dma_start(phenos_sb[:], phenos.rearrange("(o t) p -> o (t p)", o=1))
+
+        addend = held.tile([1, PAIRS], F32, name="addend")
+        nc.vector.tensor_tensor(addend[:], phenos_sb[:, 0:PAIRS], phenos_sb[:, PAIRS : 2 * PAIRS], ADD)
+        nc.vector.tensor_scalar_add(addend[:], addend[:], BC2)
+
+        h = []
+        for piece in range(2 * HALVES):
+            bank = psum.tile([D, PIECE], F32, name=f"h{piece}", tag="bank")
+            piece_offsets = offsets[:, piece * (PIECE // 16) : (piece + 1) * (PIECE // 16)]
+            nc.tensor.matmul(bank[:], w_sb[:], table_sb[:].indirect(piece_offsets), start=True, stop=True)
+            h.append(bank)
+
+        e0 = held.tile([D, PAIRS], BF16, name="e0")
+        e1 = held.tile([D, PAIRS], F32, name="e1")
+        for half in range(HALVES):
+            cols = slice(half * PIECE, (half + 1) * PIECE)
+            nc.scalar.activation(e0[:, cols], h[half][:], RELU, bias=b1_sb[:])
+            nc.vector.tensor_scalar(e1[:, cols], h[HALVES + half][:], b1_sb[:], 0.0, ADD, MAX)
+
+        out_sb = held.tile([1, PAIRS], F32, name="out_sb")
+        for half in range(HALVES):
+            cols = slice(half * PIECE, (half + 1) * PIECE)
+            q = psum.tile([D, PIECE], F32, name="q", tag="bank")
+            nc.tensor.matmul(q[:], bd_sb[:], e0[:, cols], start=True, stop=True)
+            product = work.tile([D, PIECE], F32, name="product")
+            nc.vector.tensor_tensor(product[:], q[:], e1[:, cols], MULT)
+            z = work.tile([D, PIECE], BF16, name="z")
+            nc.vector.tensor_scalar_add(z[:], product[:], boff_sb[:])
+            u = psum.tile([D, PIECE], F32, name="u", tag="bank")
+            nc.tensor.matmul(u[:], wc1_sb[:], z[:], start=True, stop=True)
+            y = work.tile([D, PIECE], BF16, name="y")
+            nc.scalar.activation(y[:], u[:], RELU, bias=bc1_sb[:])
+            score = psum.tile([1, PIECE], F32, name="score", tag="bank")
+            nc.tensor.matmul(score[:], wc2_sb[:], y[:], start=True, stop=True)
+            nc.vector.tensor_tensor(out_sb[:, cols], score[:], addend[:, cols], ADD)
+
+        nc.sync.dma_start(out, out_sb[:])

@@ -8,7 +8,10 @@ D = 128
 GENES = 1024
 PAIRS = 1024
 PIECE = 512
-HALVES = PAIRS // PIECE
+BLOCKS = 4
+BLOCK = PAIRS // BLOCKS
+STRIP = D // BLOCKS
+WARMUP = 17
 BC2 = 0.25
 
 FLOPS = 2 * D * D * (2 * PAIRS) + 2 * (2 * D * D * PAIRS) + 2 * D * PAIRS
@@ -18,63 +21,79 @@ def tile_recovermodel_kernel(tc, table, w, b1, bd, boff, wc1, bc1, wc2, phenos, 
     nc = tc.nc
     with (
         tc.tile_pool(name="held", bufs=1) as held,
-        tc.tile_pool(name="work", bufs=2) as work,
+        tc.tile_pool(name="work", bufs=BLOCKS) as work,
         tc.psum_pool(name="psum", bufs=8) as psum,
     ):
+        zeros = held.tile([D, D], BF16, name="zeros")
+        nc.gpsimd.memset(zeros[:], 0.0)
+        warm = psum.tile([D, D], F32, name="warm", tag="bank")
+        for step in range(WARMUP):
+            nc.tensor.matmul(warm[:], zeros[:], zeros[:], start=True, stop=True)
+
         offsets = held.tile([D, 2 * PAIRS // 16], U16, name="offsets")
         nc.sync.dma_start(offsets[:], offs)
         table_sb = held.tile([D, GENES], BF16, name="table_sb")
-        nc.sync.dma_start(table_sb[:], table)
+        nc.scalar.dma_start(table_sb[:], table)
         w_sb = held.tile([D, D], BF16, name="w_sb")
-        nc.scalar.dma_start(w_sb[:], w)
+        nc.sync.dma_start(w_sb[:], w)
+        b1_sb = held.tile([D, 1], F32, name="b1_sb")
+        nc.sync.dma_start(b1_sb[:], b1)
         bd_sb = held.tile([D, D], BF16, name="bd_sb")
-        nc.scalar.dma_start(bd_sb[:], bd)
+        nc.sync.dma_start(bd_sb[:], bd)
+        boff_sb = held.tile([D, 1], F32, name="boff_sb")
+        nc.sync.dma_start(boff_sb[:], boff)
         wc1_sb = held.tile([D, D], BF16, name="wc1_sb")
         nc.scalar.dma_start(wc1_sb[:], wc1)
-        b1_sb = held.tile([D, 1], F32, name="b1_sb")
-        nc.gpsimd.dma_start(b1_sb[:], b1)
-        boff_sb = held.tile([D, 1], F32, name="boff_sb")
-        nc.gpsimd.dma_start(boff_sb[:], boff)
         bc1_sb = held.tile([D, 1], F32, name="bc1_sb")
-        nc.gpsimd.dma_start(bc1_sb[:], bc1)
+        nc.scalar.dma_start(bc1_sb[:], bc1)
         wc2_sb = held.tile([D, 1], BF16, name="wc2_sb")
-        nc.gpsimd.dma_start(wc2_sb[:], wc2)
-        phenos_sb = held.tile([1, 2 * PAIRS], F32, name="phenos_sb")
-        nc.gpsimd.dma_start(phenos_sb[:], phenos.rearrange("(o t) p -> o (t p)", o=1))
-
-        addend = held.tile([1, PAIRS], F32, name="addend")
-        nc.vector.tensor_tensor(addend[:], phenos_sb[:, 0:PAIRS], phenos_sb[:, PAIRS : 2 * PAIRS], ADD)
-        nc.vector.tensor_scalar_add(addend[:], addend[:], BC2)
-
-        h = []
-        for piece in range(2 * HALVES):
-            bank = psum.tile([D, PIECE], F32, name=f"h{piece}", tag="bank")
-            piece_offsets = offsets[:, piece * (PIECE // 16) : (piece + 1) * (PIECE // 16)]
-            nc.tensor.matmul(bank[:], w_sb[:], table_sb[:].indirect(piece_offsets), start=True, stop=True)
-            h.append(bank)
+        nc.scalar.dma_start(wc2_sb[:], wc2)
+        phenos_sb = held.tile([D, 2, BLOCK], F32, name="phenos_sb")
+        nc.gpsimd.memset(phenos_sb[:], 0.0)
+        nc.sync.dma_start(
+            phenos_sb[:].rearrange("(b r) t c -> b r t c", r=STRIP)[:, 0],
+            phenos.rearrange("t (b c) -> b t c", b=BLOCKS),
+        )
 
         e0 = held.tile([D, PAIRS], BF16, name="e0")
         e1 = held.tile([D, PAIRS], F32, name="e1")
-        for half in range(HALVES):
-            cols = slice(half * PIECE, (half + 1) * PIECE)
-            nc.scalar.activation(e0[:, cols], h[half][:], RELU, bias=b1_sb[:])
-            nc.vector.tensor_scalar(e1[:, cols], h[HALVES + half][:], b1_sb[:], 0.0, ADD, MAX)
+        h = {}
+        for piece in (0, 2, 1, 3):
+            h[piece] = psum.tile([D, PIECE], F32, name=f"h{piece}", tag="bank")
+            piece_offsets = offsets[:, piece * (PIECE // 16) : (piece + 1) * (PIECE // 16)]
+            nc.tensor.matmul(h[piece][:], w_sb[:], table_sb[:].indirect(piece_offsets), start=True, stop=True)
+        nc.scalar.activation(e0[:, 0:PIECE], h[0][:], RELU, bias=b1_sb[:])
+        nc.vector.tensor_scalar(e1[:, 0:PIECE], h[2][:], b1_sb[:], 0.0, ADD, MAX)
+        nc.vector.tensor_scalar(e0[:, PIECE:PAIRS], h[1][:], b1_sb[:], 0.0, ADD, MAX)
+        nc.scalar.activation(e1[:, PIECE:PAIRS], h[3][:], RELU, bias=b1_sb[:])
 
-        out_sb = held.tile([1, PAIRS], F32, name="out_sb")
-        for half in range(HALVES):
-            cols = slice(half * PIECE, (half + 1) * PIECE)
-            q = psum.tile([D, PIECE], F32, name="q", tag="bank")
-            nc.tensor.matmul(q[:], bd_sb[:], e0[:, cols], start=True, stop=True)
-            product = work.tile([D, PIECE], F32, name="product")
-            nc.vector.tensor_tensor(product[:], q[:], e1[:, cols], MULT)
-            z = work.tile([D, PIECE], BF16, name="z")
+        wc2_strip = held.tile([D, STRIP], BF16, name="wc2_strip")
+        nc.gpsimd.tensor_copy(wc2_strip[:], wc2_sb[:, 0:1].to_broadcast([D, STRIP]))
+        addend = held.tile([D, BLOCK], F32, name="addend")
+        nc.gpsimd.tensor_tensor(addend[:], phenos_sb[:, 0, :], phenos_sb[:, 1, :], ADD)
+        nc.gpsimd.tensor_scalar_add(addend[:], addend[:], BC2)
+
+        blocks = [slice(b * BLOCK, (b + 1) * BLOCK) for b in range(BLOCKS)]
+        q, u = [], []
+        for b in range(BLOCKS):
+            q.append(psum.tile([D, BLOCK], F32, name=f"q{b}", tag="bank"))
+            nc.tensor.matmul(q[b][:], bd_sb[:], e0[:, blocks[b]], start=True, stop=True)
+        for b in range(BLOCKS):
+            product = work.tile([D, BLOCK], F32, name="product")
+            nc.vector.tensor_tensor(product[:], q[b][:], e1[:, blocks[b]], MULT)
+            z = work.tile([D, BLOCK], BF16, name="z")
             nc.vector.tensor_scalar_add(z[:], product[:], boff_sb[:])
-            u = psum.tile([D, PIECE], F32, name="u", tag="bank")
-            nc.tensor.matmul(u[:], wc1_sb[:], z[:], start=True, stop=True)
-            y = work.tile([D, PIECE], BF16, name="y")
-            nc.scalar.activation(y[:], u[:], RELU, bias=bc1_sb[:])
-            score = psum.tile([1, PIECE], F32, name="score", tag="bank")
-            nc.tensor.matmul(score[:], wc2_sb[:], y[:], start=True, stop=True)
-            nc.vector.tensor_tensor(out_sb[:, cols], score[:], addend[:, cols], ADD)
+            u.append(psum.tile([D, BLOCK], F32, name=f"u{b}", tag="bank"))
+            nc.tensor.matmul(u[b][:], wc1_sb[:], z[:], start=True, stop=True)
+        score = psum.tile([D, BLOCK], F32, name="score", tag="bank")
+        for b in range(BLOCKS):
+            y = work.tile([D, BLOCK], BF16, name="y")
+            nc.scalar.activation(y[:], u[b][:], RELU, bias=bc1_sb[:])
+            nc.tensor.matmul(score[b * STRIP : (b + 1) * STRIP, :], wc2_strip[:], y[:], start=True, stop=True)
 
-        nc.sync.dma_start(out, out_sb[:])
+        out_sb = held.tile([D, BLOCK], F32, name="out_sb")
+        nc.vector.tensor_tensor(out_sb[:], score[:], addend[:], ADD)
+        nc.sync.dma_start(
+            out.rearrange("o (b c) -> (o b) c", b=BLOCKS),
+            out_sb[:].rearrange("(b r) c -> b r c", r=STRIP)[:, 0],
+        )

@@ -10,7 +10,6 @@ PAIRS = 1024
 PIECE = 512
 BLOCKS = 4
 BLOCK = PAIRS // BLOCKS
-STRIP = D // BLOCKS
 WARMUP = 17
 BC2 = 0.25
 
@@ -26,6 +25,8 @@ def tile_recovermodel_kernel(tc, table, w, b1, bd, boff, wc1, bc1, wc2, phenos, 
     ):
         zeros = held.tile([D, D], BF16, name="zeros")
         nc.gpsimd.memset(zeros[:], 0.0)
+        wc2_in_column = held.tile([D, BLOCKS, BLOCKS], BF16, name="wc2_in_column")
+        nc.gpsimd.memset(wc2_in_column[:], 0.0)
         warm = psum.tile([D, D], F32, name="warm", tag="bank")
         for step in range(WARMUP):
             nc.tensor.matmul(warm[:], zeros[:], zeros[:], start=True, stop=True)
@@ -48,12 +49,14 @@ def tile_recovermodel_kernel(tc, table, w, b1, bd, boff, wc1, bc1, wc2, phenos, 
         nc.scalar.dma_start(bc1_sb[:], bc1)
         wc2_sb = held.tile([D, 1], BF16, name="wc2_sb")
         nc.scalar.dma_start(wc2_sb[:], wc2)
-        phenos_sb = held.tile([D, 2, BLOCK], F32, name="phenos_sb")
-        nc.gpsimd.memset(phenos_sb[:], 0.0)
-        nc.sync.dma_start(
-            phenos_sb[:].rearrange("(b r) t c -> b r t c", r=STRIP)[:, 0],
-            phenos.rearrange("t (b c) -> b t c", b=BLOCKS),
-        )
+        phenos_sb = held.tile([BLOCKS, 2, BLOCK], F32, name="phenos_sb")
+        nc.sync.dma_start(phenos_sb[:], phenos.rearrange("t (b c) -> b t c", b=BLOCKS))
+
+        for b in range(BLOCKS):
+            nc.vector.tensor_copy(wc2_in_column[:, b, b : b + 1], wc2_sb[:])
+        addend = held.tile([BLOCKS, BLOCK], F32, name="addend")
+        nc.vector.tensor_tensor(addend[:], phenos_sb[:, 0, :], phenos_sb[:, 1, :], ADD)
+        nc.vector.tensor_scalar_add(addend[:], addend[:], BC2)
 
         e0 = held.tile([D, PAIRS], BF16, name="e0")
         e1 = held.tile([D, PAIRS], F32, name="e1")
@@ -67,11 +70,6 @@ def tile_recovermodel_kernel(tc, table, w, b1, bd, boff, wc1, bc1, wc2, phenos, 
         nc.vector.tensor_scalar(e0[:, PIECE:PAIRS], h[1][:], b1_sb[:], 0.0, ADD, MAX)
         nc.scalar.activation(e1[:, PIECE:PAIRS], h[3][:], RELU, bias=b1_sb[:])
 
-        wc2_strip = held.tile([D, STRIP], BF16, name="wc2_strip")
-        nc.gpsimd.tensor_copy(wc2_strip[:], wc2_sb[:, 0:1].to_broadcast([D, STRIP]))
-        addend = held.tile([D, BLOCK], F32, name="addend")
-        nc.gpsimd.tensor_tensor(addend[:], phenos_sb[:, 0, :], phenos_sb[:, 1, :], ADD)
-        nc.gpsimd.tensor_scalar_add(addend[:], addend[:], BC2)
 
         blocks = [slice(b * BLOCK, (b + 1) * BLOCK) for b in range(BLOCKS)]
         q, u = [], []
@@ -85,15 +83,12 @@ def tile_recovermodel_kernel(tc, table, w, b1, bd, boff, wc1, bc1, wc2, phenos, 
             nc.vector.tensor_scalar_add(z[:], product[:], boff_sb[:])
             u.append(psum.tile([D, BLOCK], F32, name=f"u{b}", tag="bank"))
             nc.tensor.matmul(u[b][:], wc1_sb[:], z[:], start=True, stop=True)
-        score = psum.tile([D, BLOCK], F32, name="score", tag="bank")
+        score = psum.tile([BLOCKS, BLOCK], F32, name="score", tag="bank")
         for b in range(BLOCKS):
             y = work.tile([D, BLOCK], BF16, name="y")
             nc.scalar.activation(y[:], u[b][:], RELU, bias=bc1_sb[:])
-            nc.tensor.matmul(score[b * STRIP : (b + 1) * STRIP, :], wc2_strip[:], y[:], start=True, stop=True)
+            nc.tensor.matmul(score[:], wc2_in_column[:, b, :], y[:], start=(b == 0), stop=(b == BLOCKS - 1))
 
-        out_sb = held.tile([D, BLOCK], F32, name="out_sb")
+        out_sb = held.tile([BLOCKS, BLOCK], F32, name="out_sb")
         nc.vector.tensor_tensor(out_sb[:], score[:], addend[:], ADD)
-        nc.sync.dma_start(
-            out.rearrange("o (b c) -> (o b) c", b=BLOCKS),
-            out_sb[:].rearrange("(b r) c -> b r c", r=STRIP)[:, 0],
-        )
+        nc.sync.dma_start(out.rearrange("o (b c) -> (o b) c", b=BLOCKS), out_sb[:])

@@ -10,7 +10,6 @@ PAIRS = 1024
 PIECE = 512
 BLOCKS = 4
 BLOCK = PAIRS // BLOCKS
-WARMUP = 17
 BC2 = 0.25
 
 FLOPS = 2 * D * D * (2 * PAIRS) + 2 * (2 * D * D * PAIRS) + 2 * D * PAIRS
@@ -23,13 +22,8 @@ def tile_recovermodel_kernel(tc, table, w, b1, bd, boff, wc1, bc1, wc2, phenos, 
         tc.tile_pool(name="work", bufs=BLOCKS) as work,
         tc.psum_pool(name="psum", bufs=8) as psum,
     ):
-        zeros = held.tile([D, D], BF16, name="zeros")
-        nc.gpsimd.memset(zeros[:], 0.0)
         wc2_in_column = held.tile([D, BLOCKS, BLOCKS], BF16, name="wc2_in_column")
         nc.gpsimd.memset(wc2_in_column[:], 0.0)
-        warm = psum.tile([D, D], F32, name="warm", tag="bank")
-        for step in range(WARMUP):
-            nc.tensor.matmul(warm[:], zeros[:], zeros[:], start=True, stop=True)
 
         offsets = held.tile([D, 2 * PAIRS // 16], U16, name="offsets")
         nc.sync.dma_start(offsets[:], offs)

@@ -10,6 +10,7 @@ PAIRS = 1024
 PIECE = 512
 BLOCKS = 4
 BLOCK = PAIRS // BLOCKS
+WARMUP = 17
 BC2 = 0.25
 
 FLOPS = 2 * D * D * (2 * PAIRS) + 2 * (2 * D * D * PAIRS) + 2 * D * PAIRS
@@ -22,8 +23,15 @@ def tile_recovermodel_kernel(tc, table, w, b1, bd, boff, wc1, bc1, wc2, phenos, 
         tc.tile_pool(name="work", bufs=BLOCKS) as work,
         tc.psum_pool(name="psum", bufs=8) as psum,
     ):
+        stir = held.tile([D, D], BF16, name="stir")
+        stir_pairs = stir[:].rearrange("p (c two) -> p c two", two=2)
+        nc.vector.memset(stir_pairs[:, :, 0], 1.0)
+        nc.vector.memset(stir_pairs[:, :, 1], -1.0)
         wc2_in_column = held.tile([D, BLOCKS, BLOCKS], BF16, name="wc2_in_column")
         nc.gpsimd.memset(wc2_in_column[:], 0.0)
+        warm = psum.tile([D, D], F32, name="warm", tag="bank")
+        for step in range(WARMUP):
+            nc.tensor.matmul(warm[:], stir[:], stir[:], start=True, stop=True)
 
         offsets = held.tile([D, 2 * PAIRS // 16], U16, name="offsets")
         nc.sync.dma_start(offsets[:], offs)

@@ -8,9 +8,8 @@ D = 128
 GENES = 1024
 PAIRS = 1024
 PIECE = 512
-BLOCKS = 4
+BLOCKS = 8
 BLOCK = PAIRS // BLOCKS
-WARMUP = 17
 BC2 = 0.25
 
 FLOPS = 2 * D * D * (2 * PAIRS) + 2 * (2 * D * D * PAIRS) + 2 * D * PAIRS
@@ -23,15 +22,8 @@ def tile_recovermodel_kernel(tc, table, w, b1, bd, boff, wc1, bc1, wc2, phenos, 
         tc.tile_pool(name="work", bufs=BLOCKS) as work,
         tc.psum_pool(name="psum", bufs=8) as psum,
     ):
-        stir = held.tile([D, D], BF16, name="stir")
-        stir_pairs = stir[:].rearrange("p (c two) -> p c two", two=2)
-        nc.vector.memset(stir_pairs[:, :, 0], 1.0)
-        nc.vector.memset(stir_pairs[:, :, 1], -1.0)
         wc2_in_column = held.tile([D, BLOCKS, BLOCKS], BF16, name="wc2_in_column")
         nc.gpsimd.memset(wc2_in_column[:], 0.0)
-        warm = psum.tile([D, D], F32, name="warm", tag="bank")
-        for step in range(WARMUP):
-            nc.tensor.matmul(warm[:], stir[:], stir[:], start=True, stop=True)
 
         offsets = held.tile([D, 2 * PAIRS // 16], U16, name="offsets")
         nc.sync.dma_start(offsets[:], offs)
@@ -39,8 +31,12 @@ def tile_recovermodel_kernel(tc, table, w, b1, bd, boff, wc1, bc1, wc2, phenos, 
         nc.scalar.dma_start(table_sb[:], table)
         w_sb = held.tile([D, D], BF16, name="w_sb")
         nc.sync.dma_start(w_sb[:], w)
+        wc2_sb = held.tile([D, 1], BF16, name="wc2_sb")
+        nc.scalar.dma_start(wc2_sb[:], wc2)
         b1_sb = held.tile([D, 1], F32, name="b1_sb")
         nc.sync.dma_start(b1_sb[:], b1)
+        phenos_sb = held.tile([BLOCKS, 2, BLOCK], F32, name="phenos_sb")
+        nc.sync.dma_start(phenos_sb[:], phenos.rearrange("t (b c) -> b t c", b=BLOCKS))
         bd_sb = held.tile([D, D], BF16, name="bd_sb")
         nc.sync.dma_start(bd_sb[:], bd)
         boff_sb = held.tile([D, 1], F32, name="boff_sb")
@@ -49,16 +45,11 @@ def tile_recovermodel_kernel(tc, table, w, b1, bd, boff, wc1, bc1, wc2, phenos, 
         nc.scalar.dma_start(wc1_sb[:], wc1)
         bc1_sb = held.tile([D, 1], F32, name="bc1_sb")
         nc.scalar.dma_start(bc1_sb[:], bc1)
-        wc2_sb = held.tile([D, 1], BF16, name="wc2_sb")
-        nc.scalar.dma_start(wc2_sb[:], wc2)
-        phenos_sb = held.tile([BLOCKS, 2, BLOCK], F32, name="phenos_sb")
-        nc.sync.dma_start(phenos_sb[:], phenos.rearrange("t (b c) -> b t c", b=BLOCKS))
 
-        for b in range(BLOCKS):
-            nc.vector.tensor_copy(wc2_in_column[:, b, b : b + 1], wc2_sb[:])
+        diagonal = wc2_in_column[:].rearrange("p b m -> p (b m)")[:, 0 : BLOCKS * BLOCKS : BLOCKS + 1]
+        nc.vector.tensor_copy(diagonal, wc2_sb[:, 0:1].to_broadcast([D, BLOCKS]))
         addend = held.tile([BLOCKS, BLOCK], F32, name="addend")
-        nc.vector.tensor_tensor(addend[:], phenos_sb[:, 0, :], phenos_sb[:, 1, :], ADD)
-        nc.vector.tensor_scalar_add(addend[:], addend[:], BC2)
+        nc.vector.scalar_tensor_tensor(addend[:], phenos_sb[:, 0, :], BC2, phenos_sb[:, 1, :], ADD, ADD)
 
         e0 = held.tile([D, PAIRS], BF16, name="e0")
         e1 = held.tile([D, PAIRS], F32, name="e1")

@@ -32,7 +32,7 @@ def tile_recovermodel_kernel(tc, table, w, b1, bd, boff, wc1, bc1, wc2, phenos, 
         w_sb = held.tile([D, D], BF16, name="w_sb")
         nc.sync.dma_start(w_sb[:], w)
         wc2_sb = held.tile([D, 1], BF16, name="wc2_sb")
-        nc.scalar.dma_start(wc2_sb[:], wc2)
+        nc.sync.dma_start(wc2_sb[:], wc2)
         b1_sb = held.tile([D, 1], F32, name="b1_sb")
         nc.sync.dma_start(b1_sb[:], b1)
         phenos_sb = held.tile([BLOCKS, 2, BLOCK], F32, name="phenos_sb")
@@ -42,9 +42,9 @@ def tile_recovermodel_kernel(tc, table, w, b1, bd, boff, wc1, bc1, wc2, phenos, 
         boff_sb = held.tile([D, 1], F32, name="boff_sb")
         nc.sync.dma_start(boff_sb[:], boff)
         wc1_sb = held.tile([D, D], BF16, name="wc1_sb")
-        nc.scalar.dma_start(wc1_sb[:], wc1)
+        nc.sync.dma_start(wc1_sb[:], wc1)
         bc1_sb = held.tile([D, 1], F32, name="bc1_sb")
-        nc.scalar.dma_start(bc1_sb[:], bc1)
+        nc.sync.dma_start(bc1_sb[:], bc1)
 
         diagonal = wc2_in_column[:].rearrange("p b m -> p (b m)")[:, 0 : BLOCKS * BLOCKS : BLOCKS + 1]
         nc.vector.tensor_copy(diagonal, wc2_sb[:, 0:1].to_broadcast([D, BLOCKS]))

@@ -29,6 +29,10 @@ def tile_recovermodel_kernel(tc, table, w, b1, bd, boff, wc1, bc1, wc2, phenos, 
         nc.sync.dma_start(offsets[:], offs)
         table_sb = held.tile([D, GENES], BF16, name="table_sb")
         nc.scalar.dma_start(table_sb[:], table)
+        zero_column = held.tile([D, 1], F32, name="zero_column")
+        nc.gpsimd.memset(zero_column[:], 0.0)
+        unused_column = held.tile([D, 1], F32, name="unused_column")
+        nc.scalar.activation(unused_column[:], zero_column[:], RELU)
         w_sb = held.tile([D, D], BF16, name="w_sb")
         nc.sync.dma_start(w_sb[:], w)
         wc2_sb = held.tile([D, 1], BF16, name="wc2_sb")

@@ -1,7 +1,7 @@
 import concourse.mybir as mybir
 
 BF16, F32, U16 = mybir.dt.bfloat16, mybir.dt.float32, mybir.dt.uint16
-RELU = mybir.ActivationFunctionType.Relu
+RELU, IDENTITY = mybir.ActivationFunctionType.Relu, mybir.ActivationFunctionType.Identity
 ADD, MULT, MAX = mybir.AluOpType.add, mybir.AluOpType.mult, mybir.AluOpType.max
 
 D = 128
@@ -10,6 +10,7 @@ PAIRS = 1024
 PIECE = 512
 BLOCKS = 8
 BLOCK = PAIRS // BLOCKS
+Q_AHEAD = 6
 BC2 = 0.25
 
 FLOPS = 2 * D * D * (2 * PAIRS) + 2 * (2 * D * D * PAIRS) + 2 * D * PAIRS
@@ -45,6 +46,8 @@ def tile_recovermodel_kernel(tc, table, w, b1, bd, boff, wc1, bc1, wc2, phenos, 
         nc.sync.dma_start(bd_sb[:], bd)
         boff_sb = held.tile([D, 1], F32, name="boff_sb")
         nc.sync.dma_start(boff_sb[:], boff)
+        boff_bf = held.tile([D, 1], BF16, name="boff_bf")
+        nc.gpsimd.tensor_copy(boff_bf[:], boff_sb[:])
         wc1_sb = held.tile([D, D], BF16, name="wc1_sb")
         nc.sync.dma_start(wc1_sb[:], wc1)
         bc1_sb = held.tile([D, 1], F32, name="bc1_sb")
@@ -70,20 +73,28 @@ def tile_recovermodel_kernel(tc, table, w, b1, bd, boff, wc1, bc1, wc2, phenos, 
 
         blocks = [slice(b * BLOCK, (b + 1) * BLOCK) for b in range(BLOCKS)]
         q, u = [], []
-        for b in range(BLOCKS):
+
+        def q_matmul(b):
             q.append(psum.tile([D, BLOCK], F32, name=f"q{b}", tag="bank"))
             nc.tensor.matmul(q[b][:], bd_sb[:], e0[:, blocks[b]], start=True, stop=True)
+
+        for b in range(Q_AHEAD):
+            q_matmul(b)
+        boff_through_wc1 = psum.tile([D, 1], F32, name="boff_through_wc1", tag="bank")
+        nc.tensor.matmul(boff_through_wc1[:], wc1_sb[:], boff_bf[:], start=True, stop=True)
+        bias_u = held.tile([D, 1], F32, name="bias_u")
+        nc.scalar.activation(bias_u[:], boff_through_wc1[:], IDENTITY, bias=bc1_sb[:])
         for b in range(BLOCKS):
-            product = work.tile([D, BLOCK], F32, name="product")
+            product = work.tile([D, BLOCK], BF16, name="product")
             nc.vector.tensor_tensor(product[:], q[b][:], e1[:, blocks[b]], MULT)
-            z = work.tile([D, BLOCK], BF16, name="z")
-            nc.vector.tensor_scalar_add(z[:], product[:], boff_sb[:])
             u.append(psum.tile([D, BLOCK], F32, name=f"u{b}", tag="bank"))
-            nc.tensor.matmul(u[b][:], wc1_sb[:], z[:], start=True, stop=True)
+            nc.tensor.matmul(u[b][:], wc1_sb[:], product[:], start=True, stop=True)
+            if b + Q_AHEAD < BLOCKS:
+                q_matmul(b + Q_AHEAD)
         score = psum.tile([BLOCKS, BLOCK], F32, name="score", tag="bank")
         for b in range(BLOCKS):
             y = work.tile([D, BLOCK], BF16, name="y")
-            nc.scalar.activation(y[:], u[b][:], RELU, bias=bc1_sb[:])
+            nc.scalar.activation(y[:], u[b][:], RELU, bias=bias_u[:])
             nc.tensor.matmul(score[:], wc2_in_column[:, b, :], y[:], start=(b == 0), stop=(b == BLOCKS - 1))
 
         out_sb = held.tile([BLOCKS, BLOCK], F32, name="out_sb")

@@ -23,40 +23,38 @@ def tile_recovermodel_kernel(tc, table, w, b1, bd, boff, wc1, bc1, wc2, phenos, 
         tc.tile_pool(name="work", bufs=BLOCKS) as work,
         tc.psum_pool(name="psum", bufs=8) as psum,
     ):
-        wc2_in_column = held.tile([D, BLOCKS, BLOCKS], BF16, name="wc2_in_column")
-        nc.gpsimd.memset(wc2_in_column[:], 0.0)
-
-        offsets = held.tile([D, 2 * PAIRS // 16], U16, name="offsets")
-        nc.sync.dma_start(offsets[:], offs)
-        table_sb = held.tile([D, GENES], BF16, name="table_sb")
-        nc.scalar.dma_start(table_sb[:], table)
         zero_column = held.tile([D, 1], F32, name="zero_column")
         nc.gpsimd.memset(zero_column[:], 0.0)
         unused_column = held.tile([D, 1], F32, name="unused_column")
         nc.scalar.activation(unused_column[:], zero_column[:], RELU)
+
+        table_sb = held.tile([D, GENES], BF16, name="table_sb")
+        nc.sync.dma_start(table_sb[:], table)
+        offsets = held.tile([D, 2 * PAIRS // 16], U16, name="offsets")
+        nc.sync.dma_start(offsets[:], offs)
         w_sb = held.tile([D, D], BF16, name="w_sb")
         nc.sync.dma_start(w_sb[:], w)
-        wc2_sb = held.tile([D, 1], BF16, name="wc2_sb")
-        nc.sync.dma_start(wc2_sb[:], wc2)
         b1_sb = held.tile([D, 1], F32, name="b1_sb")
         nc.sync.dma_start(b1_sb[:], b1)
-        phenos_sb = held.tile([BLOCKS, 2, BLOCK], F32, name="phenos_sb")
-        nc.sync.dma_start(phenos_sb[:], phenos.rearrange("t (b c) -> b t c", b=BLOCKS))
         bd_sb = held.tile([D, D], BF16, name="bd_sb")
         nc.sync.dma_start(bd_sb[:], bd)
         boff_sb = held.tile([D, 1], F32, name="boff_sb")
         nc.sync.dma_start(boff_sb[:], boff)
-        boff_bf = held.tile([D, 1], BF16, name="boff_bf")
-        nc.gpsimd.tensor_copy(boff_bf[:], boff_sb[:])
         wc1_sb = held.tile([D, D], BF16, name="wc1_sb")
         nc.sync.dma_start(wc1_sb[:], wc1)
         bc1_sb = held.tile([D, 1], F32, name="bc1_sb")
         nc.sync.dma_start(bc1_sb[:], bc1)
+        wc2_sb = held.tile([D, 1], BF16, name="wc2_sb")
+        nc.sync.dma_start(wc2_sb[:], wc2)
+        phenos_sb = held.tile([BLOCKS, 2, BLOCK], F32, name="phenos_sb")
+        nc.sync.dma_start(phenos_sb[:], phenos.rearrange("t (b c) -> b t c", b=BLOCKS))
 
+        wc2_in_column = held.tile([D, BLOCKS, BLOCKS], BF16, name="wc2_in_column")
+        nc.gpsimd.memset(wc2_in_column[:], 0.0)
+        boff_bf = held.tile([D, 1], BF16, name="boff_bf")
+        nc.gpsimd.tensor_copy(boff_bf[:], boff_sb[:])
         diagonal = wc2_in_column[:].rearrange("p b m -> p (b m)")[:, 0 : BLOCKS * BLOCKS : BLOCKS + 1]
-        nc.vector.tensor_copy(diagonal, wc2_sb[:, 0:1].to_broadcast([D, BLOCKS]))
-        addend = held.tile([BLOCKS, BLOCK], F32, name="addend")
-        nc.vector.scalar_tensor_tensor(addend[:], phenos_sb[:, 0, :], BC2, phenos_sb[:, 1, :], ADD, ADD)
+        nc.gpsimd.tensor_copy(diagonal, wc2_sb[:, 0:1].to_broadcast([D, BLOCKS]))
 
         e0 = held.tile([D, PAIRS], BF16, name="e0")
         e1 = held.tile([D, PAIRS], F32, name="e1")
@@ -91,6 +89,8 @@ def tile_recovermodel_kernel(tc, table, w, b1, bd, boff, wc1, bc1, wc2, phenos, 
             nc.tensor.matmul(u[b][:], wc1_sb[:], product[:], start=True, stop=True)
             if b + Q_AHEAD < BLOCKS:
                 q_matmul(b + Q_AHEAD)
+        addend = held.tile([BLOCKS, BLOCK], F32, name="addend")
+        nc.vector.scalar_tensor_tensor(addend[:], phenos_sb[:, 0, :], BC2, phenos_sb[:, 1, :], ADD, ADD)
         score = psum.tile([BLOCKS, BLOCK], F32, name="score", tag="bank")
         for b in range(BLOCKS):
             y = work.tile([D, BLOCK], BF16, name="y")

@@ -8,9 +8,9 @@ D = 128
 GENES = 1024
 PAIRS = 1024
 PIECE = 512
-BLOCKS = 8
-BLOCK = PAIRS // BLOCKS
-Q_AHEAD = 6
+ROWS = 8
+ROW = PAIRS // ROWS
+WIDTHS = (ROW, ROW, 2 * ROW, 2 * ROW, ROW, ROW)
 BC2 = 0.25
 
 FLOPS = 2 * D * D * (2 * PAIRS) + 2 * (2 * D * D * PAIRS) + 2 * D * PAIRS
@@ -20,7 +20,7 @@ def tile_recovermodel_kernel(tc, table, w, b1, bd, boff, wc1, bc1, wc2, phenos, 
     nc = tc.nc
     with (
         tc.tile_pool(name="held", bufs=1) as held,
-        tc.tile_pool(name="work", bufs=BLOCKS) as work,
+        tc.tile_pool(name="work", bufs=len(WIDTHS)) as work,
         tc.psum_pool(name="psum", bufs=8) as psum,
     ):
         zero_column = held.tile([D, 1], F32, name="zero_column")
@@ -46,15 +46,15 @@ def tile_recovermodel_kernel(tc, table, w, b1, bd, boff, wc1, bc1, wc2, phenos, 
         nc.sync.dma_start(bc1_sb[:], bc1)
         wc2_sb = held.tile([D, 1], BF16, name="wc2_sb")
         nc.sync.dma_start(wc2_sb[:], wc2)
-        phenos_sb = held.tile([BLOCKS, 2, BLOCK], F32, name="phenos_sb")
-        nc.sync.dma_start(phenos_sb[:], phenos.rearrange("t (b c) -> b t c", b=BLOCKS))
+        phenos_sb = held.tile([ROWS, 2, ROW], F32, name="phenos_sb")
+        nc.sync.dma_start(phenos_sb[:], phenos.rearrange("t (r c) -> r t c", r=ROWS))
 
-        wc2_in_column = held.tile([D, BLOCKS, BLOCKS], BF16, name="wc2_in_column")
+        wc2_in_column = held.tile([D, ROWS, ROWS], BF16, name="wc2_in_column")
         nc.gpsimd.memset(wc2_in_column[:], 0.0)
         boff_bf = held.tile([D, 1], BF16, name="boff_bf")
         nc.gpsimd.tensor_copy(boff_bf[:], boff_sb[:])
-        diagonal = wc2_in_column[:].rearrange("p b m -> p (b m)")[:, 0 : BLOCKS * BLOCKS : BLOCKS + 1]
-        nc.gpsimd.tensor_copy(diagonal, wc2_sb[:, 0:1].to_broadcast([D, BLOCKS]))
+        diagonal = wc2_in_column[:].rearrange("p r m -> p (r m)")[:, 0 : ROWS * ROWS : ROWS + 1]
+        nc.gpsimd.tensor_copy(diagonal, wc2_sb[:, 0:1].to_broadcast([D, ROWS]))
 
         e0 = held.tile([D, PAIRS], BF16, name="e0")
         e1 = held.tile([D, PAIRS], F32, name="e1")
@@ -69,34 +69,32 @@ def tile_recovermodel_kernel(tc, table, w, b1, bd, boff, wc1, bc1, wc2, phenos, 
         nc.scalar.activation(e1[:, PIECE:PAIRS], h[3][:], RELU, bias=b1_sb[:])
 
 
-        blocks = [slice(b * BLOCK, (b + 1) * BLOCK) for b in range(BLOCKS)]
+        starts = [sum(WIDTHS[:b]) for b in range(len(WIDTHS))]
+        blocks = [slice(start, start + width) for start, width in zip(starts, WIDTHS)]
         q, u = [], []
-
-        def q_matmul(b):
-            q.append(psum.tile([D, BLOCK], F32, name=f"q{b}", tag="bank"))
+        for b, width in enumerate(WIDTHS):
+            q.append(psum.tile([D, width], F32, name=f"q{b}", tag="bank"))
             nc.tensor.matmul(q[b][:], bd_sb[:], e0[:, blocks[b]], start=True, stop=True)
-
-        for b in range(Q_AHEAD):
-            q_matmul(b)
         boff_through_wc1 = psum.tile([D, 1], F32, name="boff_through_wc1", tag="bank")
         nc.tensor.matmul(boff_through_wc1[:], wc1_sb[:], boff_bf[:], start=True, stop=True)
         bias_u = held.tile([D, 1], F32, name="bias_u")
         nc.scalar.activation(bias_u[:], boff_through_wc1[:], IDENTITY, bias=bc1_sb[:])
-        for b in range(BLOCKS):
-            product = work.tile([D, BLOCK], BF16, name="product")
+        for b, width in enumerate(WIDTHS):
+            product = work.tile([D, width], BF16, name="product")
             nc.vector.tensor_tensor(product[:], q[b][:], e1[:, blocks[b]], MULT)
-            u.append(psum.tile([D, BLOCK], F32, name=f"u{b}", tag="bank"))
+            u.append(psum.tile([D, width], F32, name=f"u{b}", tag="bank"))
             nc.tensor.matmul(u[b][:], wc1_sb[:], product[:], start=True, stop=True)
-            if b + Q_AHEAD < BLOCKS:
-                q_matmul(b + Q_AHEAD)
-        addend = held.tile([BLOCKS, BLOCK], F32, name="addend")
+        addend = held.tile([ROWS, ROW], F32, name="addend")
         nc.vector.scalar_tensor_tensor(addend[:], phenos_sb[:, 0, :], BC2, phenos_sb[:, 1, :], ADD, ADD)
-        score = psum.tile([BLOCKS, BLOCK], F32, name="score", tag="bank")
-        for b in range(BLOCKS):
-            y = work.tile([D, BLOCK], BF16, name="y")
+        score = psum.tile([ROWS, ROW], F32, name="score", tag="bank")
+        for b, width in enumerate(WIDTHS):
+            y = work.tile([D, width], BF16, name="y")
             nc.scalar.activation(y[:], u[b][:], RELU, bias=bias_u[:])
-            nc.tensor.matmul(score[:], wc2_in_column[:, b, :], y[:], start=(b == 0), stop=(b == BLOCKS - 1))
+            for i in range(width // ROW):
+                r = starts[b] // ROW + i
+                y_row = y[:, i * ROW : (i + 1) * ROW]
+                nc.tensor.matmul(score[:], wc2_in_column[:, r, :], y_row, start=(r == 0), stop=(r == ROWS - 1))
 
-        out_sb = held.tile([BLOCKS, BLOCK], F32, name="out_sb")
+        out_sb = held.tile([ROWS, ROW], F32, name="out_sb")
         nc.vector.tensor_tensor(out_sb[:], score[:], addend[:], ADD)
-        nc.sync.dma_start(out.rearrange("o (b c) -> (o b) c", b=BLOCKS), out_sb[:])
+        nc.sync.dma_start(out.rearrange("o (r c) -> (o r) c", r=ROWS), out_sb[:])

@@ -1,7 +1,7 @@
 import concourse.mybir as mybir
 
 BF16, F32, U16 = mybir.dt.bfloat16, mybir.dt.float32, mybir.dt.uint16
-RELU, IDENTITY = mybir.ActivationFunctionType.Relu, mybir.ActivationFunctionType.Identity
+RELU = mybir.ActivationFunctionType.Relu
 ADD, MULT, MAX = mybir.AluOpType.add, mybir.AluOpType.mult, mybir.AluOpType.max
 
 D = 128
@@ -75,10 +75,11 @@ def tile_recovermodel_kernel(tc, table, w, b1, bd, boff, wc1, bc1, wc2, phenos, 
         for b, width in enumerate(WIDTHS):
             q.append(psum.tile([D, width], F32, name=f"q{b}", tag="bank"))
             nc.tensor.matmul(q[b][:], bd_sb[:], e0[:, blocks[b]], start=True, stop=True)
-        boff_through_wc1 = psum.tile([D, 1], F32, name="boff_through_wc1", tag="bank")
-        nc.tensor.matmul(boff_through_wc1[:], wc1_sb[:], boff_bf[:], start=True, stop=True)
+            if b == 0:
+                boff_through_wc1 = psum.tile([D, 1], F32, name="boff_through_wc1", tag="bank")
+                nc.tensor.matmul(boff_through_wc1[:], wc1_sb[:], boff_bf[:], start=True, stop=True)
         bias_u = held.tile([D, 1], F32, name="bias_u")
-        nc.scalar.activation(bias_u[:], boff_through_wc1[:], IDENTITY, bias=bc1_sb[:])
+        nc.vector.tensor_tensor(bias_u[:], boff_through_wc1[:], bc1_sb[:], ADD)
         for b, width in enumerate(WIDTHS):
             product = work.tile([D, width], BF16, name="product")
             nc.vector.tensor_tensor(product[:], q[b][:], e1[:, blocks[b]], MULT)
@@ -89,7 +90,10 @@ def tile_recovermodel_kernel(tc, table, w, b1, bd, boff, wc1, bc1, wc2, phenos, 
         score = psum.tile([ROWS, ROW], F32, name="score", tag="bank")
         for b, width in enumerate(WIDTHS):
             y = work.tile([D, width], BF16, name="y")
-            nc.scalar.activation(y[:], u[b][:], RELU, bias=bias_u[:])
+            if b < len(WIDTHS) - 1:
+                nc.scalar.activation(y[:], u[b][:], RELU, bias=bias_u[:])
+            else:
+                nc.vector.tensor_scalar(y[:], u[b][:], bias_u[:], 0.0, ADD, MAX)
             for i in range(width // ROW):
                 r = starts[b] // ROW + i
                 y_row = y[:, i * ROW : (i + 1) * ROW]

@@ -10,7 +10,7 @@ PAIRS = 1024
 PIECE = 512
 ROWS = 8
 ROW = PAIRS // ROWS
-WIDTHS = (ROW, ROW, 2 * ROW, 2 * ROW, ROW, ROW)
+Q_WIDTHS = (ROW, ROW, 2 * ROW, 4 * ROW)
 BC2 = 0.25
 
 FLOPS = 2 * D * D * (2 * PAIRS) + 2 * (2 * D * D * PAIRS) + 2 * D * PAIRS
@@ -20,7 +20,7 @@ def tile_recovermodel_kernel(tc, table, w, b1, bd, boff, wc1, bc1, wc2, phenos, 
     nc = tc.nc
     with (
         tc.tile_pool(name="held", bufs=1) as held,
-        tc.tile_pool(name="work", bufs=len(WIDTHS)) as work,
+        tc.tile_pool(name="work", bufs=ROWS) as work,
         tc.psum_pool(name="psum", bufs=8) as psum,
     ):
         zero_column = held.tile([D, 1], F32, name="zero_column")
@@ -44,10 +44,10 @@ def tile_recovermodel_kernel(tc, table, w, b1, bd, boff, wc1, bc1, wc2, phenos, 
         nc.sync.dma_start(wc1_sb[:], wc1)
         bc1_sb = held.tile([D, 1], F32, name="bc1_sb")
         nc.sync.dma_start(bc1_sb[:], bc1)
-        wc2_sb = held.tile([D, 1], BF16, name="wc2_sb")
-        nc.sync.dma_start(wc2_sb[:], wc2)
         phenos_sb = held.tile([ROWS, 2, ROW], F32, name="phenos_sb")
         nc.sync.dma_start(phenos_sb[:], phenos.rearrange("t (r c) -> r t c", r=ROWS))
+        wc2_sb = held.tile([D, 1], BF16, name="wc2_sb")
+        nc.sync.dma_start(wc2_sb[:], wc2)
 
         wc2_in_column = held.tile([D, ROWS, ROWS], BF16, name="wc2_in_column")
         nc.gpsimd.memset(wc2_in_column[:], 0.0)
@@ -69,35 +69,31 @@ def tile_recovermodel_kernel(tc, table, w, b1, bd, boff, wc1, bc1, wc2, phenos, 
         nc.scalar.activation(e1[:, PIECE:PAIRS], h[3][:], RELU, bias=b1_sb[:])
 
 
-        starts = [sum(WIDTHS[:b]) for b in range(len(WIDTHS))]
-        blocks = [slice(start, start + width) for start, width in zip(starts, WIDTHS)]
         q, u = [], []
-        for b, width in enumerate(WIDTHS):
-            q.append(psum.tile([D, width], F32, name=f"q{b}", tag="bank"))
-            nc.tensor.matmul(q[b][:], bd_sb[:], e0[:, blocks[b]], start=True, stop=True)
-            if b == 0:
+        for start, width in zip((0, ROW, 2 * ROW, 4 * ROW), Q_WIDTHS):
+            q_bank = psum.tile([D, width], F32, name=f"q_from_{start}", tag="bank")
+            nc.tensor.matmul(q_bank[:], bd_sb[:], e0[:, start : start + width], start=True, stop=True)
+            q += [q_bank[:, c : c + ROW] for c in range(0, width, ROW)]
+            if start == 0:
                 boff_through_wc1 = psum.tile([D, 1], F32, name="boff_through_wc1", tag="bank")
                 nc.tensor.matmul(boff_through_wc1[:], wc1_sb[:], boff_bf[:], start=True, stop=True)
         bias_u = held.tile([D, 1], F32, name="bias_u")
         nc.vector.tensor_tensor(bias_u[:], boff_through_wc1[:], bc1_sb[:], ADD)
-        for b, width in enumerate(WIDTHS):
-            product = work.tile([D, width], BF16, name="product")
-            nc.vector.tensor_tensor(product[:], q[b][:], e1[:, blocks[b]], MULT)
-            u.append(psum.tile([D, width], F32, name=f"u{b}", tag="bank"))
-            nc.tensor.matmul(u[b][:], wc1_sb[:], product[:], start=True, stop=True)
+        for r in range(ROWS):
+            product = work.tile([D, ROW], BF16, name="product")
+            nc.vector.tensor_tensor(product[:], q[r], e1[:, r * ROW : (r + 1) * ROW], MULT)
+            u.append(psum.tile([D, ROW], F32, name=f"u{r}", tag="bank"))
+            nc.tensor.matmul(u[r][:], wc1_sb[:], product[:], start=True, stop=True)
         addend = held.tile([ROWS, ROW], F32, name="addend")
         nc.vector.scalar_tensor_tensor(addend[:], phenos_sb[:, 0, :], BC2, phenos_sb[:, 1, :], ADD, ADD)
         score = psum.tile([ROWS, ROW], F32, name="score", tag="bank")
-        for b, width in enumerate(WIDTHS):
-            y = work.tile([D, width], BF16, name="y")
-            if b < len(WIDTHS) - 1:
-                nc.scalar.activation(y[:], u[b][:], RELU, bias=bias_u[:])
+        for r in range(ROWS):
+            y = work.tile([D, ROW], BF16, name="y")
+            if r < ROWS - 2:
+                nc.scalar.activation(y[:], u[r][:], RELU, bias=bias_u[:])
             else:
-                nc.vector.tensor_scalar(y[:], u[b][:], bias_u[:], 0.0, ADD, MAX)
-            for i in range(width // ROW):
-                r = starts[b] // ROW + i
-                y_row = y[:, i * ROW : (i + 1) * ROW]
-                nc.tensor.matmul(score[:], wc2_in_column[:, r, :], y_row, start=(r == 0), stop=(r == ROWS - 1))
+                nc.vector.tensor_scalar(y[:], u[r][:], bias_u[:], 0.0, ADD, MAX)
+            nc.tensor.matmul(score[:], wc2_in_column[:, r, :], y[:], start=(r == 0), stop=(r == ROWS - 1))
 
         out_sb = held.tile([ROWS, ROW], F32, name="out_sb")
         nc.vector.tensor_tensor(out_sb[:], score[:], addend[:], ADD)

@@ -8,9 +8,11 @@ D = 128
 GENES = 1024
 PAIRS = 1024
 PIECE = 512
-ROWS = 8
+ROWS = 16
 ROW = PAIRS // ROWS
-Q_WIDTHS = (ROW, ROW, 2 * ROW, 4 * ROW)
+Q_WIDTHS = (2 * ROW, 2 * ROW, 4 * ROW, 4 * ROW, 4 * ROW)
+WIDTHS = 7 * (2 * ROW,) + 2 * (ROW,)
+STARTS = [sum(WIDTHS[:b]) for b in range(len(WIDTHS))]
 BC2 = 0.25
 
 FLOPS = 2 * D * D * (2 * PAIRS) + 2 * (2 * D * D * PAIRS) + 2 * D * PAIRS
@@ -20,7 +22,7 @@ def tile_recovermodel_kernel(tc, table, w, b1, bd, boff, wc1, bc1, wc2, phenos, 
     nc = tc.nc
     with (
         tc.tile_pool(name="held", bufs=1) as held,
-        tc.tile_pool(name="work", bufs=ROWS) as work,
+        tc.tile_pool(name="work", bufs=len(WIDTHS)) as work,
         tc.psum_pool(name="psum", bufs=8) as psum,
     ):
         zero_column = held.tile([D, 1], F32, name="zero_column")
@@ -69,31 +71,38 @@ def tile_recovermodel_kernel(tc, table, w, b1, bd, boff, wc1, bc1, wc2, phenos, 
         nc.scalar.activation(e1[:, PIECE:PAIRS], h[3][:], RELU, bias=b1_sb[:])
 
 
-        q, u = [], []
-        for start, width in zip((0, ROW, 2 * ROW, 4 * ROW), Q_WIDTHS):
+        q, u = {}, []
+        for j, width in enumerate(Q_WIDTHS):
+            start = sum(Q_WIDTHS[:j])
             q_bank = psum.tile([D, width], F32, name=f"q_from_{start}", tag="bank")
             nc.tensor.matmul(q_bank[:], bd_sb[:], e0[:, start : start + width], start=True, stop=True)
-            q += [q_bank[:, c : c + ROW] for c in range(0, width, ROW)]
-            if start == 0:
+            for block_start, block_width in zip(STARTS, WIDTHS):
+                if start <= block_start < start + width:
+                    q[block_start] = q_bank[:, block_start - start : block_start - start + block_width]
+            if j == 0:
                 boff_through_wc1 = psum.tile([D, 1], F32, name="boff_through_wc1", tag="bank")
                 nc.tensor.matmul(boff_through_wc1[:], wc1_sb[:], boff_bf[:], start=True, stop=True)
         bias_u = held.tile([D, 1], F32, name="bias_u")
         nc.vector.tensor_tensor(bias_u[:], boff_through_wc1[:], bc1_sb[:], ADD)
-        for r in range(ROWS):
-            product = work.tile([D, ROW], BF16, name="product")
-            nc.vector.tensor_tensor(product[:], q[r], e1[:, r * ROW : (r + 1) * ROW], MULT)
-            u.append(psum.tile([D, ROW], F32, name=f"u{r}", tag="bank"))
-            nc.tensor.matmul(u[r][:], wc1_sb[:], product[:], start=True, stop=True)
+        for b, (start, width) in enumerate(zip(STARTS, WIDTHS)):
+            product = work.tile([D, width], BF16, name="product")
+            nc.vector.tensor_tensor(product[:], q[start], e1[:, start : start + width], MULT)
+            u.append(psum.tile([D, width], F32, name=f"u{b}", tag="bank"))
+            nc.tensor.matmul(u[b][:], wc1_sb[:], product[:], start=True, stop=True)
         addend = held.tile([ROWS, ROW], F32, name="addend")
         nc.vector.scalar_tensor_tensor(addend[:], phenos_sb[:, 0, :], BC2, phenos_sb[:, 1, :], ADD, ADD)
         score = psum.tile([ROWS, ROW], F32, name="score", tag="bank")
-        for r in range(ROWS):
-            y = work.tile([D, ROW], BF16, name="y")
-            if r < ROWS - 2:
-                nc.scalar.activation(y[:], u[r][:], RELU, bias=bias_u[:])
+        last = len(WIDTHS) - 1
+        for b, (start, width) in enumerate(zip(STARTS, WIDTHS)):
+            y = work.tile([D, width], BF16, name="y")
+            if b in (last - 2, last):
+                nc.vector.tensor_scalar(y[:], u[b][:], bias_u[:], 0.0, ADD, MAX)
             else:
-                nc.vector.tensor_scalar(y[:], u[r][:], bias_u[:], 0.0, ADD, MAX)
-            nc.tensor.matmul(score[:], wc2_in_column[:, r, :], y[:], start=(r == 0), stop=(r == ROWS - 1))
+                nc.scalar.activation(y[:], u[b][:], RELU, bias=bias_u[:])
+            for i in range(width // ROW):
+                r = start // ROW + i
+                y_row = y[:, i * ROW : (i + 1) * ROW]
+                nc.tensor.matmul(score[:], wc2_in_column[:, r, :], y_row, start=(r == 0), stop=(r == ROWS - 1))
 
         out_sb = held.tile([ROWS, ROW], F32, name="out_sb")
         nc.vector.tensor_tensor(out_sb[:], score[:], addend[:], ADD)

@@ -8,6 +8,8 @@ D = 128
 GENES = 1024
 PAIRS = 1024
 PIECE = 512
+HALF = PIECE // 2
+PIECES = ((0, PIECE), (PAIRS, PIECE), (PIECE, PIECE), (PAIRS + PIECE, HALF), (PAIRS + PIECE + HALF, HALF))
 ROWS = 16
 ROW = PAIRS // ROWS
 Q_WIDTHS = (2 * ROW, 2 * ROW, 4 * ROW, 4 * ROW, 4 * ROW)
@@ -61,27 +63,32 @@ def tile_recovermodel_kernel(tc, table, w, b1, bd, boff, wc1, bc1, wc2, phenos, 
         e0 = held.tile([D, PAIRS], BF16, name="e0")
         e1 = held.tile([D, PAIRS], F32, name="e1")
         h = {}
-        for piece in (0, 2, 1, 3):
-            h[piece] = psum.tile([D, PIECE], F32, name=f"h{piece}", tag="bank")
-            piece_offsets = offsets[:, piece * (PIECE // 16) : (piece + 1) * (PIECE // 16)]
-            nc.tensor.matmul(h[piece][:], w_sb[:], table_sb[:].indirect(piece_offsets), start=True, stop=True)
+        for first, entries in PIECES:
+            h[first] = psum.tile([D, entries], F32, name=f"h_from_{first}", tag="bank")
+            piece_offsets = offsets[:, first // 16 : (first + entries) // 16]
+            nc.tensor.matmul(h[first][:], w_sb[:], table_sb[:].indirect(piece_offsets), start=True, stop=True)
         nc.scalar.activation(e0[:, 0:PIECE], h[0][:], RELU, bias=b1_sb[:])
-        nc.vector.tensor_scalar(e1[:, 0:PIECE], h[2][:], b1_sb[:], 0.0, ADD, MAX)
-        nc.vector.tensor_scalar(e0[:, PIECE:PAIRS], h[1][:], b1_sb[:], 0.0, ADD, MAX)
-        nc.scalar.activation(e1[:, PIECE:PAIRS], h[3][:], RELU, bias=b1_sb[:])
-
+        nc.vector.tensor_scalar(e1[:, 0:PIECE], h[PAIRS][:], b1_sb[:], 0.0, ADD, MAX)
+        nc.vector.tensor_scalar(e0[:, PIECE:PAIRS], h[PIECE][:], b1_sb[:], 0.0, ADD, MAX)
+        for first in (PIECE, PIECE + HALF):
+            nc.scalar.activation(e1[:, first : first + HALF], h[PAIRS + first][:], RELU, bias=b1_sb[:])
 
         q, u = {}, []
-        for j, width in enumerate(Q_WIDTHS):
-            start = sum(Q_WIDTHS[:j])
+
+        def q_matmul(j):
+            start, width = sum(Q_WIDTHS[:j]), Q_WIDTHS[j]
             q_bank = psum.tile([D, width], F32, name=f"q_from_{start}", tag="bank")
             nc.tensor.matmul(q_bank[:], bd_sb[:], e0[:, start : start + width], start=True, stop=True)
             for block_start, block_width in zip(STARTS, WIDTHS):
                 if start <= block_start < start + width:
                     q[block_start] = q_bank[:, block_start - start : block_start - start + block_width]
-            if j == 0:
-                boff_through_wc1 = psum.tile([D, 1], F32, name="boff_through_wc1", tag="bank")
-                nc.tensor.matmul(boff_through_wc1[:], wc1_sb[:], boff_bf[:], start=True, stop=True)
+
+        q_matmul(0)
+        boff_through_wc1 = psum.tile([D, 1], F32, name="boff_through_wc1", tag="bank")
+        nc.tensor.matmul(boff_through_wc1[:], wc1_sb[:], boff_bf[:], start=True, stop=True)
+        last_q = len(Q_WIDTHS) - 1
+        for j in range(1, last_q):
+            q_matmul(j)
         bias_u = held.tile([D, 1], F32, name="bias_u")
         nc.vector.tensor_tensor(bias_u[:], boff_through_wc1[:], bc1_sb[:], ADD)
         for b, (start, width) in enumerate(zip(STARTS, WIDTHS)):
@@ -89,6 +96,8 @@ def tile_recovermodel_kernel(tc, table, w, b1, bd, boff, wc1, bc1, wc2, phenos, 
             nc.vector.tensor_tensor(product[:], q[start], e1[:, start : start + width], MULT)
             u.append(psum.tile([D, width], F32, name=f"u{b}", tag="bank"))
             nc.tensor.matmul(u[b][:], wc1_sb[:], product[:], start=True, stop=True)
+            if b == 0:
+                q_matmul(last_q)
         addend = held.tile([ROWS, ROW], F32, name="addend")
         nc.vector.scalar_tensor_tensor(addend[:], phenos_sb[:, 0, :], BC2, phenos_sb[:, 1, :], ADD, ADD)
         score = psum.tile([ROWS, ROW], F32, name="score", tag="bank")

@@ -15,6 +15,7 @@ ROW = PAIRS // ROWS
 Q_WIDTHS = (2 * ROW, 2 * ROW, 4 * ROW, 4 * ROW, 4 * ROW)
 WIDTHS = 7 * (2 * ROW,) + 2 * (ROW,)
 STARTS = [sum(WIDTHS[:b]) for b in range(len(WIDTHS))]
+HALF_WAY = 4
 BC2 = 0.25
 
 FLOPS = 2 * D * D * (2 * PAIRS) + 2 * (2 * D * D * PAIRS) + 2 * D * PAIRS
@@ -101,10 +102,9 @@ def tile_recovermodel_kernel(tc, table, w, b1, bd, boff, wc1, bc1, wc2, phenos, 
         addend = held.tile([ROWS, ROW], F32, name="addend")
         nc.vector.scalar_tensor_tensor(addend[:], phenos_sb[:, 0, :], BC2, phenos_sb[:, 1, :], ADD, ADD)
         score = psum.tile([ROWS, ROW], F32, name="score", tag="bank")
-        last = len(WIDTHS) - 1
         for b, (start, width) in enumerate(zip(STARTS, WIDTHS)):
             y = work.tile([D, width], BF16, name="y")
-            if b in (last - 2, last):
+            if b >= HALF_WAY and b % 2 == 0:
                 nc.vector.tensor_scalar(y[:], u[b][:], bias_u[:], 0.0, ADD, MAX)
             else:
                 nc.scalar.activation(y[:], u[b][:], RELU, bias=bias_u[:])

@@ -58,6 +58,8 @@ def tile_recovermodel_kernel(tc, table, w, b1, bd, boff, wc1, bc1, wc2, phenos, 
         nc.gpsimd.memset(wc2_in_column[:], 0.0)
         boff_bf = held.tile([D, 1], BF16, name="boff_bf")
         nc.gpsimd.tensor_copy(boff_bf[:], boff_sb[:])
+        phenos_sum = held.tile([ROWS, ROW], F32, name="phenos_sum")
+        nc.gpsimd.tensor_tensor(phenos_sum[:], phenos_sb[:, 0, :], phenos_sb[:, 1, :], ADD)
         diagonal = wc2_in_column[:].rearrange("p r m -> p (r m)")[:, 0 : ROWS * ROWS : ROWS + 1]
         nc.gpsimd.tensor_copy(diagonal, wc2_sb[:, 0:1].to_broadcast([D, ROWS]))
 
@@ -99,8 +101,6 @@ def tile_recovermodel_kernel(tc, table, w, b1, bd, boff, wc1, bc1, wc2, phenos, 
             nc.tensor.matmul(u[b][:], wc1_sb[:], product[:], start=True, stop=True)
             if b == 0:
                 q_matmul(last_q)
-        addend = held.tile([ROWS, ROW], F32, name="addend")
-        nc.vector.scalar_tensor_tensor(addend[:], phenos_sb[:, 0, :], BC2, phenos_sb[:, 1, :], ADD, ADD)
         score = psum.tile([ROWS, ROW], F32, name="score", tag="bank")
         for b, (start, width) in enumerate(zip(STARTS, WIDTHS)):
             y = work.tile([D, width], BF16, name="y")
@@ -114,5 +114,5 @@ def tile_recovermodel_kernel(tc, table, w, b1, bd, boff, wc1, bc1, wc2, phenos, 
                 nc.tensor.matmul(score[:], wc2_in_column[:, r, :], y_row, start=(r == 0), stop=(r == ROWS - 1))
 
         out_sb = held.tile([ROWS, ROW], F32, name="out_sb")
-        nc.vector.tensor_tensor(out_sb[:], score[:], addend[:], ADD)
+        nc.vector.scalar_tensor_tensor(out_sb[:], score[:], BC2, phenos_sum[:], ADD, ADD)
         nc.sync.dma_start(out.rearrange("o (r c) -> (o r) c", r=ROWS), out_sb[:])

import concourse.mybir as mybir

BF16, F32, U16 = mybir.dt.bfloat16, mybir.dt.float32, mybir.dt.uint16
RELU = mybir.ActivationFunctionType.Relu
ADD, MULT, MAX = mybir.AluOpType.add, mybir.AluOpType.mult, mybir.AluOpType.max

D = 128
GENES = 1024
PAIRS = 1024
PIECE = 512
HALF = PIECE // 2
PIECES = ((0, PIECE), (PAIRS, PIECE), (PIECE, PIECE), (PAIRS + PIECE, HALF), (PAIRS + PIECE + HALF, HALF))
ROWS = 16
ROW = PAIRS // ROWS
Q_WIDTHS = (2 * ROW, 2 * ROW, 4 * ROW, 4 * ROW, 4 * ROW)
WIDTHS = 7 * (2 * ROW,) + 2 * (ROW,)
STARTS = [sum(WIDTHS[:b]) for b in range(len(WIDTHS))]
HALF_WAY = 4
BC2 = 0.25

FLOPS = 2 * D * D * (2 * PAIRS) + 2 * (2 * D * D * PAIRS) + 2 * D * PAIRS


def tile_recovermodel_kernel(tc, table, w, b1, bd, boff, wc1, bc1, wc2, phenos, offs, out):
    nc = tc.nc
    with (
        tc.tile_pool(name="held", bufs=1) as held,
        tc.tile_pool(name="work", bufs=len(WIDTHS)) as work,
        tc.psum_pool(name="psum", bufs=8) as psum,
    ):
        zero_column = held.tile([D, 1], F32, name="zero_column")
        nc.gpsimd.memset(zero_column[:], 0.0)
        unused_column = held.tile([D, 1], F32, name="unused_column")
        nc.scalar.activation(unused_column[:], zero_column[:], RELU)

        table_sb = held.tile([D, GENES], BF16, name="table_sb")
        nc.sync.dma_start(table_sb[:], table)
        offsets = held.tile([D, 2 * PAIRS // 16], U16, name="offsets")
        nc.sync.dma_start(offsets[:], offs)
        w_sb = held.tile([D, D], BF16, name="w_sb")
        nc.sync.dma_start(w_sb[:], w)
        b1_sb = held.tile([D, 1], F32, name="b1_sb")
        nc.sync.dma_start(b1_sb[:], b1)
        bd_sb = held.tile([D, D], BF16, name="bd_sb")
        nc.sync.dma_start(bd_sb[:], bd)
        boff_sb = held.tile([D, 1], F32, name="boff_sb")
        nc.sync.dma_start(boff_sb[:], boff)
        wc1_sb = held.tile([D, D], BF16, name="wc1_sb")
        nc.sync.dma_start(wc1_sb[:], wc1)
        bc1_sb = held.tile([D, 1], F32, name="bc1_sb")
        nc.sync.dma_start(bc1_sb[:], bc1)
        phenos_sb = held.tile([ROWS, 2, ROW], F32, name="phenos_sb")
        nc.sync.dma_start(phenos_sb[:], phenos.rearrange("t (r c) -> r t c", r=ROWS))
        wc2_sb = held.tile([D, 1], BF16, name="wc2_sb")
        nc.sync.dma_start(wc2_sb[:], wc2)

        wc2_in_column = held.tile([D, ROWS, ROWS], BF16, name="wc2_in_column")
        nc.gpsimd.memset(wc2_in_column[:], 0.0)
        boff_bf = held.tile([D, 1], BF16, name="boff_bf")
        nc.gpsimd.tensor_copy(boff_bf[:], boff_sb[:])
        phenos_sum = held.tile([ROWS, ROW], F32, name="phenos_sum")
        nc.gpsimd.tensor_tensor(phenos_sum[:], phenos_sb[:, 0, :], phenos_sb[:, 1, :], ADD)
        diagonal = wc2_in_column[:].rearrange("p r m -> p (r m)")[:, 0 : ROWS * ROWS : ROWS + 1]
        nc.gpsimd.tensor_copy(diagonal, wc2_sb[:, 0:1].to_broadcast([D, ROWS]))

        e0 = held.tile([D, PAIRS], BF16, name="e0")
        e1 = held.tile([D, PAIRS], F32, name="e1")
        h = {}
        for first, entries in PIECES:
            h[first] = psum.tile([D, entries], F32, name=f"h_from_{first}", tag="bank")
            piece_offsets = offsets[:, first // 16 : (first + entries) // 16]
            nc.tensor.matmul(h[first][:], w_sb[:], table_sb[:].indirect(piece_offsets), start=True, stop=True)
        nc.scalar.activation(e0[:, 0:PIECE], h[0][:], RELU, bias=b1_sb[:])
        nc.vector.tensor_scalar(e1[:, 0:PIECE], h[PAIRS][:], b1_sb[:], 0.0, ADD, MAX)
        nc.vector.tensor_scalar(e0[:, PIECE:PAIRS], h[PIECE][:], b1_sb[:], 0.0, ADD, MAX)
        for first in (PIECE, PIECE + HALF):
            nc.scalar.activation(e1[:, first : first + HALF], h[PAIRS + first][:], RELU, bias=b1_sb[:])

        q, u = {}, []

        def q_matmul(j):
            start, width = sum(Q_WIDTHS[:j]), Q_WIDTHS[j]
            q_bank = psum.tile([D, width], F32, name=f"q_from_{start}", tag="bank")
            nc.tensor.matmul(q_bank[:], bd_sb[:], e0[:, start : start + width], start=True, stop=True)
            for block_start, block_width in zip(STARTS, WIDTHS):
                if start <= block_start < start + width:
                    q[block_start] = q_bank[:, block_start - start : block_start - start + block_width]

        q_matmul(0)
        boff_through_wc1 = psum.tile([D, 1], F32, name="boff_through_wc1", tag="bank")
        nc.tensor.matmul(boff_through_wc1[:], wc1_sb[:], boff_bf[:], start=True, stop=True)
        last_q = len(Q_WIDTHS) - 1
        for j in range(1, last_q):
            q_matmul(j)
        bias_u = held.tile([D, 1], F32, name="bias_u")
        nc.vector.tensor_tensor(bias_u[:], boff_through_wc1[:], bc1_sb[:], ADD)
        for b, (start, width) in enumerate(zip(STARTS, WIDTHS)):
            product = work.tile([D, width], BF16, name="product")
            nc.vector.tensor_tensor(product[:], q[start], e1[:, start : start + width], MULT)
            u.append(psum.tile([D, width], F32, name=f"u{b}", tag="bank"))
            nc.tensor.matmul(u[b][:], wc1_sb[:], product[:], start=True, stop=True)
            if b == 0:
                q_matmul(last_q)
        score = psum.tile([ROWS, ROW], F32, name="score", tag="bank")
        for b, (start, width) in enumerate(zip(STARTS, WIDTHS)):
            y = work.tile([D, width], BF16, name="y")
            if b >= HALF_WAY and b % 2 == 0:
                nc.vector.tensor_scalar(y[:], u[b][:], bias_u[:], 0.0, ADD, MAX)
            else:
                nc.scalar.activation(y[:], u[b][:], RELU, bias=bias_u[:])
            for i in range(width // ROW):
                r = start // ROW + i
                y_row = y[:, i * ROW : (i + 1) * ROW]
                nc.tensor.matmul(score[:], wc2_in_column[:, r, :], y_row, start=(r == 0), stop=(r == ROWS - 1))

        out_sb = held.tile([ROWS, ROW], F32, name="out_sb")
        nc.vector.scalar_tensor_tensor(out_sb[:], score[:], BC2, phenos_sum[:], ADD, ADD)
        nc.sync.dma_start(out.rearrange("o (r c) -> (o r) c", r=ROWS), out_sb[:])
